import numpy as np
import ml_dtypes


def mxq(x, axis, fmt="e4m3"):
    dtype, down = {"e4m3": (ml_dtypes.float8_e4m3fn, 7), "e5m2": (ml_dtypes.float8_e5m2, 14)}[fmt]
    v = np.moveaxis(np.asarray(x, np.float32).astype(ml_dtypes.bfloat16).astype(np.float64), axis, -1)
    blocks = v.reshape(v.shape[:-1] + (-1, 32))
    amax = np.abs(blocks).max(-1, keepdims=True)
    byte = np.maximum(np.where(amax > 0, np.frexp(amax)[1] - 1 + 127, 0) - down, 1)
    scale = np.exp2(byte - 127.0)
    codes = (blocks / scale).astype(np.float32).astype(dtype).astype(np.float64)
    return np.moveaxis((codes * scale).reshape(v.shape), -1, axis)


WIDE = False


def mx_kscale(k):
    if not WIDE:
        return np.ones(k)
    levels = np.array([10, -10, 5, -5, 0])
    a = np.random.permutation(np.resize(levels, k // 512 * 4)).reshape(k // 512, 4)
    idx = np.arange(k)
    return np.exp2(a[idx // 512, idx % 128 // 32])


BF16 = ml_dtypes.bfloat16


def bf(x):
    return np.asarray(x, np.float32).astype(BF16)


def f64(x):
    return np.asarray(x).astype(np.float64)


B, T, D, K, CD, CF, M = 8, 16, 1024, 32, 128, 512, 256
LN_EPS = 1e-5


def setup_inputs():
    s = mx_kscale(D)
    t = mx_kscale(CF)
    return {
        "h": bf(np.random.standard_normal((B, T, D)) * s),
        "mu_w1_h": bf(np.random.standard_normal((D, CF)) / np.sqrt(D) / s[:, None]),
        "code_mu": bf(np.random.standard_normal((K, CF)) * 0.4),
        "mu_b1": bf(np.random.standard_normal(CF) * 0.2),
        "ln_g": bf((1.0 + 0.1 * np.random.standard_normal(CF)) * t),
        "ln_b": bf(np.random.standard_normal(CF) * 0.2 * t),
        "mu_w2": bf(np.random.standard_normal((CF, CF)) / np.sqrt(CF) / t[:, None]),
        "mu_b2": bf(np.random.standard_normal(CF) * 0.2),
    }


def reference(h, mu_w1_h, code_mu, mu_b1, ln_g, ln_b, mu_w2, mu_b2):
    hp = mxq(f64(h), 2, "e4m3") @ mxq(f64(mu_w1_h), 0, "e4m3")
    mu_pre = hp[:, :, None, :] + f64(code_mu) + f64(mu_b1)
    mean = mu_pre.mean(-1, keepdims=True)
    var = np.square(mu_pre - mean).mean(-1, keepdims=True)
    mu_ln = (mu_pre - mean) * (1.0 / np.sqrt(var + LN_EPS)) * f64(ln_g) + f64(ln_b)
    return np.tanh((mxq(mu_ln, 3, "e4m3") @ mxq(f64(mu_w2), 0, "e4m3")) + f64(mu_b2))

@@ -1,0 +1,366 @@
+from contextlib import ExitStack
+
+from concourse import mybir
+from concourse.masks import make_identity
+
+F32 = mybir.dt.float32
+BF16 = mybir.dt.bfloat16
+U32 = mybir.dt.uint32
+U8 = mybir.dt.uint8
+FP8X4 = mybir.dt.float8_e4m3fn_x4
+ALU = mybir.AluOpType
+ACT = mybir.ActivationFunctionType
+AX = mybir.AxisListType
+
+P = 128
+TOK = 128
+D_IN = 1024
+CF = 512
+NCODE = 32
+LN_EPS = 1e-5
+CG = 4
+ROUNDS = NCODE // CG
+W = CG * TOK
+
+FLOPS = 2 * TOK * D_IN * CF + 2 * TOK * NCODE * CF * CF
+
+ROW_B1 = 32
+ROW_G = 64
+ROW_B = 65
+ROW_B2 = 66
+
+GB_ENG = ["s","s","s","s"]
+RG_V = 320
+W1_V = 352
+
+
+def regroup(eng_copy, dst, src):
+    eng_copy(
+        out=dst.rearrange("p (c i) t -> p c t i", i=4),
+        in_=src.rearrange("p t (c i) -> p c t i", i=4),
+    )
+
+
+def tile_mixtureconfounderprior_pa_kernel(
+    tc, h, mu_w1_h, code_mu, mu_b1, ln_g, ln_b, mu_w2, mu_b2, out
+):
+    nc = tc.nc
+    h2 = h.rearrange("b t d -> (b t) d")
+    out3 = out.rearrange("b t k n -> (b t) k n")
+
+    with ExitStack() as ctx:
+        keep = ctx.enter_context(tc.tile_pool(name="keep", bufs=1))
+        work = ctx.enter_context(tc.tile_pool(name="work", bufs=3))
+        psr = ctx.enter_context(tc.psum_pool(name="psr", bufs=2))
+        pso = ctx.enter_context(tc.psum_pool(name="pso", bufs=6))
+        ctx.enter_context(tc.manual_schedule())
+
+        sm_raw = keep.tile([P, CF], BF16)
+        nc.vector.memset(sm_raw[:], 0.0)
+        h_sb = keep.tile([P, D_IN], BF16)
+        nc.sync.dma_start(out=h_sb[:], in_=h2)
+        w1_raw = keep.tile([P, 2, 4, CF], BF16)
+        for g in range(2):
+            nc.sync.dma_start(
+                out=w1_raw[:, g].rearrange("p (u e) c -> p u e c", u=2),
+                in_=mu_w1_h[512 * g : 512 * (g + 1), :].rearrange(
+                    "(u p e) c -> p u e c", u=2, e=2
+                ),
+            )
+        nc.scalar.dma_start(out=sm_raw[0:NCODE, :], in_=code_mu)
+        nc.scalar.dma_start(out=sm_raw[ROW_B1 : ROW_B1 + 1, :], in_=mu_b1.unsqueeze(0))
+        nc.scalar.dma_start(out=sm_raw[ROW_G : ROW_G + 1, :], in_=ln_g.unsqueeze(0))
+        nc.scalar.dma_start(out=sm_raw[ROW_B : ROW_B + 1, :], in_=ln_b.unsqueeze(0))
+        nc.scalar.dma_start(out=sm_raw[ROW_B2 : ROW_B2 + 1, :], in_=mu_b2.unsqueeze(0))
+        w2_raw = keep.tile([P, 4, CF], BF16)
+        nc.scalar.dma_start(out=w2_raw[:], in_=mu_w2.rearrange("(t p) n -> p t n", p=P))
+
+        ident = keep.tile([P, P], F32)
+        make_identity(nc, ident[:])
+        ident_bf = keep.tile([P, P], BF16)
+        make_identity(nc, ident_bf[:])
+        ones = keep.tile([P, P], F32)
+        nc.vector.memset(ones[:], 1.0 / CF)
+        eps = keep.tile([P, 1], F32)
+        nc.vector.memset(eps[:], LN_EPS)
+        warm = keep.tile([P, 1], F32)
+        nc.scalar.activation(out=warm[:], in_=eps[:], func=ACT.Sqrt)
+
+        h_w = h_sb[:].bitcast(F32)
+        xt = pso.tile([P, 2, 2, P], F32, tag="o")
+        for g in range(2):
+            for u in range(2):
+                nc.tensor.transpose(
+                    xt[:, g, u, :], h_w[:, 256 * g + 128 * u : 256 * g + 128 * u + 128], ident[:]
+                )
+        hg = keep.tile([P, 2, TOK, 4], BF16, align_bytes=64)
+        nc.vector.tensor_copy(
+            out=hg[:].bitcast(F32), in_=xt[:].rearrange("p g u r -> p g r u")
+        )
+
+        w1g = keep.tile([P, 2, CF, 4], BF16, align_bytes=64)
+        w1_codes = keep.tile([P, 2, CF], U32, align_bytes=64)
+        w1_scales = keep.tile([P, 2, CF], U8, align_bytes=64)
+        h_codes = keep.tile([P, 2 * TOK], U32, align_bytes=64)
+        h_scales = keep.tile([P, 2 * TOK], U8, align_bytes=64)
+
+        regroup(nc.vector.tensor_copy, w1g[:, 0, 0:W1_V], w1_raw[:, 0, :, 0:W1_V])
+        regroup(nc.scalar.copy, w1g[:, 0, W1_V:CF], w1_raw[:, 0, :, W1_V:CF])
+        nc.vector.quantize_mx(
+            out=h_codes[:].bitcast(FP8X4),
+            scales=h_scales[:],
+            in_=hg[:].rearrange("p g r t -> p (g r t)"),
+        )
+        regroup(nc.vector.tensor_copy, w1g[:, 1, 0:W1_V], w1_raw[:, 1, :, 0:W1_V])
+        regroup(nc.scalar.copy, w1g[:, 1, W1_V:CF], w1_raw[:, 1, :, W1_V:CF])
+
+        smT_ps = pso.tile([P, 4, P], BF16, tag="o")
+        for t in range(4):
+            nc.tensor.transpose(smT_ps[:, t, :], sm_raw[:, P * t : P * (t + 1)], ident_bf[:])
+        smT = keep.tile([P, 4, P], F32)
+        nc.scalar.copy(out=smT[:], in_=smT_ps[:])
+
+        nc.vector.quantize_mx(
+            out=w1_codes[:, 0, :].bitcast(FP8X4),
+            scales=w1_scales[:, 0, :],
+            in_=w1g[:, 0].rearrange("p c t -> p (c t)"),
+        )
+        cm1 = keep.tile([P, 4, NCODE], F32)
+        nc.vector.tensor_tensor(
+            out=cm1[:],
+            in0=smT[:, :, 0:NCODE],
+            in1=smT[:, :, ROW_B1 : ROW_B1 + 1].to_broadcast([P, 4, NCODE]),
+            op=ALU.add,
+        )
+        mc_ps = pso.tile([P, NCODE], F32, tag="o")
+        for t in range(4):
+            nc.tensor.matmul(
+                mc_ps[:], lhsT=ones[:], rhs=cm1[:, t, :], start=(t == 0), stop=(t == 3)
+            )
+        nc.vector.quantize_mx(
+            out=w1_codes[:, 1, :].bitcast(FP8X4),
+            scales=w1_scales[:, 1, :],
+            in_=w1g[:, 1].rearrange("p c t -> p (c t)"),
+        )
+
+        hp_ps = pso.tile([P, CF], F32, tag="o")
+        for g in range(2):
+            nc.tensor.matmul_mx(
+                out=hp_ps[:],
+                lhsT=h_codes[:, TOK * g : TOK * (g + 1)].bitcast(FP8X4),
+                lhsT_scale=h_scales[:, TOK * g : TOK * (g + 1)],
+                rhs=w1_codes[:, g, :].bitcast(FP8X4),
+                rhs_scale=w1_scales[:, g, :],
+                start=(g == 0),
+                stop=(g == 1),
+            )
+        hpT_ps = pso.tile([P, 4, TOK], F32, tag="o")
+        for t in range(4):
+            for g in range(2):
+                nc.tensor.matmul_mx(
+                    out=hpT_ps[:, t, :],
+                    lhsT=w1_codes[:, g, P * t : P * (t + 1)].bitcast(FP8X4),
+                    lhsT_scale=w1_scales[:, g, P * t : P * (t + 1)],
+                    rhs=h_codes[:, TOK * g : TOK * (g + 1)].bitcast(FP8X4),
+                    rhs_scale=h_scales[:, TOK * g : TOK * (g + 1)],
+                    start=(g == 0),
+                    stop=(g == 1),
+                )
+        hpT = keep.tile([P, 4, TOK], F32)
+        nc.scalar.copy(out=hpT[:], in_=hpT_ps[:])
+
+        c_sb = keep.tile([P, 4, NCODE], F32)
+        nc.vector.tensor_tensor(
+            out=c_sb[:],
+            in0=cm1[:],
+            in1=mc_ps[:].unsqueeze(1).to_broadcast([P, 4, NCODE]),
+            op=ALU.subtract,
+        )
+        csq = keep.tile([P, 4, NCODE], F32)
+        nc.vector.tensor_tensor(out=csq[:], in0=c_sb[:], in1=c_sb[:], op=ALU.mult)
+        c2 = keep.tile([P, 4, NCODE], F32)
+        nc.vector.tensor_scalar_mul(out=c2[:], in0=c_sb[:], scalar1=2.0 / CF)
+        v_ps = pso.tile([P, NCODE], F32, tag="o")
+        for t in range(4):
+            nc.tensor.matmul(v_ps[:], lhsT=ones[:], rhs=csq[:, t, :], start=(t == 0), stop=False)
+
+        st = keep.tile([P, 6], F32)
+        nc.vector.bn_stats(out=st[:], in_=hp_ps[:])
+        mv = keep.tile([P, 2], F32)
+        nc.vector.bn_aggr(out=mv[:], in_=st[:])
+        hpc = keep.tile([P, CF], F32)
+        nc.vector.tensor_scalar(
+            out=hpc[:], in0=hp_ps[:], scalar1=mv[:, 0:1], scalar2=None, op0=ALU.subtract
+        )
+        for t in range(4):
+            nc.tensor.matmul(v_ps[:], lhsT=hpT[:, t, :], rhs=c2[:, t, :], start=False, stop=(t == 3))
+        aT_ps = pso.tile([P, 4, TOK], F32, tag="o")
+        for t in range(4):
+            nc.tensor.transpose(aT_ps[:, t, :], hpc[:, P * t : P * (t + 1)], ident[:])
+        vhe = keep.tile([P, 1], F32)
+        nc.vector.tensor_scalar_add(out=vhe[:], in0=mv[:, 1:2], scalar1=LN_EPS)
+        std = keep.tile([P, NCODE], F32)
+        nc.scalar.activation(out=std[:], in_=v_ps[:], func=ACT.Sqrt, bias=vhe[:, 0:1])
+        r_sb = keep.tile([P, NCODE], F32)
+        nc.vector.reciprocal(out=r_sb[:], in_=std[:])
+        a_sb = keep.tile([P, 4, TOK], F32)
+        nc.vector.tensor_copy(out=a_sb[:], in_=aT_ps[:])
+        nc.scalar.activation(out=warm[:], in_=eps[:], func=ACT.Tanh)
+
+        b2_ps = pso.tile([P, CF], F32, tag="o")
+        nc.tensor.matmul(
+            b2_ps[:],
+            lhsT=ident_bf[:, ROW_B2 : ROW_B2 + 1].to_broadcast([P, P]),
+            rhs=sm_raw[:],
+            start=True,
+            stop=True,
+        )
+        b2_bc = keep.tile([P, CF], F32)
+        nc.scalar.copy(out=b2_bc[:], in_=b2_ps[:])
+        w2g = keep.tile([P, CF, 4], BF16, align_bytes=64)
+        regroup(nc.scalar.copy, w2g[:], w2_raw[:])
+        w2_codes = keep.tile([P, CF], U32, align_bytes=64)
+        w2_scales = keep.tile([P, CF], U8, align_bytes=64)
+
+        tiles = {}
+
+        def bcast_r(rd):
+            for cl in range(CG):
+                code = CG * rd + cl
+                if rd == 0:
+                    r_one = pso.tile([P, TOK], F32, tag="o", name="r_one")
+                    tiles[("r", rd, cl)] = r_one[:]
+                else:
+                    if cl == 0:
+                        r_ps = psr.tile([P, CG, TOK], F32, tag="r", name="r_ps")
+                        tiles[("rt", rd)] = r_ps
+                    tiles[("r", rd, cl)] = tiles[("rt", rd)][:, cl, :]
+                nc.tensor.matmul(
+                    tiles[("r", rd, cl)],
+                    lhsT=r_sb[:, code : code + 1].to_broadcast([P, P]),
+                    rhs=ident[:],
+                    start=True,
+                    stop=True,
+                )
+
+        def normalise(rd):
+            z = work.tile([P, 4, CG, TOK], F32, name="z")
+            tiles[("z", rd)] = z
+            for cl in range(CG):
+                code = CG * rd + cl
+                for t in range(4):
+                    nc.vector.scalar_tensor_tensor(
+                        out=z[:, t, cl, :],
+                        in0=a_sb[:, t, :],
+                        scalar=c_sb[:, t, code : code + 1],
+                        in1=tiles[("r", rd, cl)],
+                        op0=ALU.add,
+                        op1=ALU.mult,
+                    )
+
+        def gain_bias(rd):
+            z = tiles[("z", rd)]
+            m = work.tile([P, 4, W], BF16, name="m")
+            tiles[("m", rd)] = m
+            for t in range(4):
+                if GB_ENG[t] == "s":
+                    nc.scalar.activation(
+                        out=m[:, t, :],
+                        in_=z[:, t].rearrange("p c r -> p (c r)"),
+                        func=ACT.Identity,
+                        scale=smT[:, t, ROW_G : ROW_G + 1],
+                        bias=smT[:, t, ROW_B : ROW_B + 1],
+                    )
+                else:
+                    nc.gpsimd.tensor_scalar(
+                        out=m[:, t, :],
+                        in0=z[:, t].rearrange("p c r -> p (c r)"),
+                        scalar1=smT[:, t, ROW_G : ROW_G + 1],
+                        scalar2=smT[:, t, ROW_B : ROW_B + 1],
+                        op0=ALU.mult,
+                        op1=ALU.add,
+                    )
+
+        def regroup_mu(rd):
+            m = tiles[("m", rd)]
+            mg = work.tile([P, W, 4], BF16, align_bytes=64, name="mg")
+            tiles[("mg", rd)] = mg
+            if RG_V > 0:
+                regroup(nc.vector.tensor_copy, mg[:, 0:RG_V], m[:, :, 0:RG_V])
+            if RG_V < W:
+                regroup(nc.scalar.copy, mg[:, RG_V:W], m[:, :, RG_V:W])
+
+        def quantise_mu(rd):
+            mg = tiles[("mg", rd)]
+            mu_codes = work.tile([P, W], U32, align_bytes=64, name="mu_codes")
+            mu_scales = work.tile([P, W], U8, align_bytes=64, name="mu_scales")
+            tiles[("q", rd)] = (mu_codes, mu_scales)
+            nc.vector.quantize_mx(
+                out=mu_codes[:].bitcast(FP8X4),
+                scales=mu_scales[:],
+                in_=mg[:].rearrange("p w t -> p (w t)"),
+            )
+
+        def second_mm(rd):
+            mu_codes, mu_scales = tiles[("q", rd)]
+            for cl in range(CG):
+                o_ps = pso.tile([P, CF], F32, tag="o", name="o_ps")
+                tiles[("o", rd, cl)] = o_ps
+                nc.tensor.matmul_mx(
+                    out=o_ps[:],
+                    lhsT=mu_codes[:, TOK * cl : TOK * (cl + 1)].bitcast(FP8X4),
+                    lhsT_scale=mu_scales[:, TOK * cl : TOK * (cl + 1)],
+                    rhs=w2_codes[:].bitcast(FP8X4),
+                    rhs_scale=w2_scales[:],
+                    start=True,
+                    stop=True,
+                )
+
+        def finish(rd, cls):
+            if cls[0] == 0:
+                res_new = work.tile([P, CG, CF], F32, name="res")
+                tiles[("res", rd)] = res_new
+            res = tiles[("res", rd)]
+            for cl in cls:
+                nc.vector.tensor_tensor(
+                    out=res[:, cl, :], in0=tiles[("o", rd, cl)][:], in1=b2_bc[:], op=ALU.add
+                )
+            for cl in cls:
+                nc.scalar.activation(out=res[:, cl, :], in_=res[:, cl, :], func=ACT.Tanh)
+
+        def store(rd, lo, hi):
+            res = tiles[("res", rd)]
+            nc.sync.dma_start(out=out3[:, CG * rd + lo : CG * rd + hi, :], in_=res[:, lo:hi, :])
+
+        bcast_r(0)
+        bcast_r(1)
+        normalise(0)
+        gain_bias(0)
+        normalise(1)
+        nc.vector.quantize_mx(
+            out=w2_codes[:].bitcast(FP8X4),
+            scales=w2_scales[:],
+            in_=w2g[:].rearrange("p c t -> p (c t)"),
+        )
+        for rd in range(ROUNDS):
+            if rd + 2 < ROUNDS:
+                bcast_r(rd + 2)
+            regroup_mu(rd)
+            if rd + 1 < ROUNDS:
+                gain_bias(rd + 1)
+            if rd > 0:
+                finish(rd - 1, [0, 1])
+            quantise_mu(rd)
+            second_mm(rd)
+            if rd > 0:
+                finish(rd - 1, [2, 3])
+                store(rd - 1, 0, CG)
+            if rd + 2 < ROUNDS:
+                normalise(rd + 2)
+        last = ROUNDS - 1
+        finish(last, [0, 1])
+        store(last, 0, 2)
+        finish(last, [2])
+        store(last, 2, 3)
+        finish(last, [3])
+        store(last, 3, 4)

@@ -29,8 +29,8 @@ ROW_G = 64
 ROW_B = 65
 ROW_B2 = 66
 
-GB_ENG = ["s","s","s","s"]
-RG_V = 320
+GB_ENG = ["g","g","g","g"]
+RG_V = 0
 W1_V = 352
 
 
@@ -332,35 +332,72 @@ def tile_mixtureconfounderprior_pa_kernel(
             res = tiles[("res", rd)]
             nc.sync.dma_start(out=out3[:, CG * rd + lo : CG * rd + hi, :], in_=res[:, lo:hi, :])
 
+        def normalise_part(rd, cls):
+            if cls[0] == 0:
+                z_new = work.tile([P, 4, CG, TOK], F32, name="z")
+                tiles[("z", rd)] = z_new
+            z = tiles[("z", rd)]
+            for cl in cls:
+                code = CG * rd + cl
+                for t in range(4):
+                    nc.vector.scalar_tensor_tensor(
+                        out=z[:, t, cl, :],
+                        in0=a_sb[:, t, :],
+                        scalar=c_sb[:, t, code : code + 1],
+                        in1=tiles[("r", rd, cl)],
+                        op0=ALU.add,
+                        op1=ALU.mult,
+                    )
+
+        def add_b2(rd, cls):
+            if cls[0] == 0:
+                res_new = work.tile([P, CG, CF], F32, name="res")
+                tiles[("res", rd)] = res_new
+            res = tiles[("res", rd)]
+            for cl in cls:
+                nc.vector.tensor_tensor(
+                    out=res[:, cl, :], in0=tiles[("o", rd, cl)][:], in1=b2_bc[:], op=ALU.add
+                )
+
+        def tanh(rd, cls):
+            res = tiles[("res", rd)]
+            for cl in cls:
+                nc.scalar.activation(out=res[:, cl, :], in_=res[:, cl, :], func=ACT.Tanh)
+
         bcast_r(0)
         bcast_r(1)
-        normalise(0)
+        normalise_part(0, [0, 1, 2, 3])
         gain_bias(0)
-        normalise(1)
+        normalise_part(1, [0, 1, 2, 3])
         nc.vector.quantize_mx(
             out=w2_codes[:].bitcast(FP8X4),
             scales=w2_scales[:],
             in_=w2g[:].rearrange("p c t -> p (c t)"),
         )
         for rd in range(ROUNDS):
-            if rd + 2 < ROUNDS:
+            more = rd + 2 < ROUNDS
+            if more:
                 bcast_r(rd + 2)
             regroup_mu(rd)
             if rd + 1 < ROUNDS:
                 gain_bias(rd + 1)
             if rd > 0:
-                finish(rd - 1, [0, 1])
+                add_b2(rd - 1, [0, 1, 2, 3])
+                tanh(rd - 1, [0, 1, 2, 3])
+                store(rd - 1, 0, CG)
+            if more:
+                normalise_part(rd + 2, [0])
             quantise_mu(rd)
             second_mm(rd)
-            if rd > 0:
-                finish(rd - 1, [2, 3])
-                store(rd - 1, 0, CG)
-            if rd + 2 < ROUNDS:
-                normalise(rd + 2)
+            if more:
+                normalise_part(rd + 2, [1,2,3])
         last = ROUNDS - 1
-        finish(last, [0, 1])
+        add_b2(last, [0, 1])
+        tanh(last, [0, 1])
         store(last, 0, 2)
-        finish(last, [2])
+        add_b2(last, [2])
+        tanh(last, [2])
         store(last, 2, 3)
-        finish(last, [3])
+        add_b2(last, [3])
+        tanh(last, [3])
         store(last, 3, 4)

@@ -25,12 +25,13 @@ W = CG * TOK
 FLOPS = 2 * TOK * D_IN * CF + 2 * TOK * NCODE * CF * CF
 
 ROW_B1 = 32
-ROW_G = 64
-ROW_B = 65
-ROW_B2 = 66
+ROW_G = 40
+ROW_B = 48
+ROW_B2 = 56
 
-GB_ENG = ["g","g","g","g"]
-RG_V = 0
+GB_ENG = [["s","s","g","g"],["g","g","g","g"],["g","g","g","g"],["g","g","g","g"],["g","g","g","g"],["g","g","g","g"],["g","g","g","g"],["g","g","g","g"]]
+RG_V = [0,0,0,0,0,256,256,256]
+LEAD = 3
 W1_V = 352
 
 
@@ -51,12 +52,11 @@ def tile_mixtureconfounderprior_pa_kernel(
     with ExitStack() as ctx:
         keep = ctx.enter_context(tc.tile_pool(name="keep", bufs=1))
         work = ctx.enter_context(tc.tile_pool(name="work", bufs=3))
+        zpool = ctx.enter_context(tc.tile_pool(name="zpool", bufs=4))
         psr = ctx.enter_context(tc.psum_pool(name="psr", bufs=2))
         pso = ctx.enter_context(tc.psum_pool(name="pso", bufs=6))
         ctx.enter_context(tc.manual_schedule())
 
-        sm_raw = keep.tile([P, CF], BF16)
-        nc.vector.memset(sm_raw[:], 0.0)
         h_sb = keep.tile([P, D_IN], BF16)
         nc.sync.dma_start(out=h_sb[:], in_=h2)
         w1_raw = keep.tile([P, 2, 4, CF], BF16)
@@ -67,18 +67,20 @@ def tile_mixtureconfounderprior_pa_kernel(
                     "(u p e) c -> p u e c", u=2, e=2
                 ),
             )
+        sm_raw = keep.tile([P, CF], BF16)
         nc.scalar.dma_start(out=sm_raw[0:NCODE, :], in_=code_mu)
-        nc.scalar.dma_start(out=sm_raw[ROW_B1 : ROW_B1 + 1, :], in_=mu_b1.unsqueeze(0))
-        nc.scalar.dma_start(out=sm_raw[ROW_G : ROW_G + 1, :], in_=ln_g.unsqueeze(0))
-        nc.scalar.dma_start(out=sm_raw[ROW_B : ROW_B + 1, :], in_=ln_b.unsqueeze(0))
-        nc.scalar.dma_start(out=sm_raw[ROW_B2 : ROW_B2 + 1, :], in_=mu_b2.unsqueeze(0))
-        w2_raw = keep.tile([P, 4, CF], BF16)
-        nc.scalar.dma_start(out=w2_raw[:], in_=mu_w2.rearrange("(t p) n -> p t n", p=P))
+        nc.scalar.dma_start(out=sm_raw[ROW_B1 : ROW_B1 + 8, :], in_=mu_b1.partition_broadcast(8))
+        nc.scalar.dma_start(out=sm_raw[ROW_G : ROW_G + 8, :], in_=ln_g.partition_broadcast(8))
+        nc.scalar.dma_start(out=sm_raw[ROW_B : ROW_B + 8, :], in_=ln_b.partition_broadcast(8))
+        nc.scalar.dma_start(out=sm_raw[ROW_B2 : ROW_B2 + 8, :], in_=mu_b2.partition_broadcast(8))
+        nc.vector.memset(sm_raw[64:128, :].bitcast(F32), 0.0)
 
         ident = keep.tile([P, P], F32)
         make_identity(nc, ident[:])
         ident_bf = keep.tile([P, P], BF16)
         make_identity(nc, ident_bf[:])
+        w2_raw = keep.tile([P, 4, CF], BF16)
+        nc.gpsimd.dma_start(out=w2_raw[:], in_=mu_w2.rearrange("(t p) n -> p t n", p=P))
         ones = keep.tile([P, P], F32)
         nc.vector.memset(ones[:], 1.0 / CF)
         eps = keep.tile([P, 1], F32)
@@ -97,6 +99,11 @@ def tile_mixtureconfounderprior_pa_kernel(
         nc.vector.tensor_copy(
             out=hg[:].bitcast(F32), in_=xt[:].rearrange("p g u r -> p g r u")
         )
+        smT_ps = pso.tile([P, 4, P], BF16, tag="o")
+        for t in range(4):
+            nc.tensor.transpose(smT_ps[:, t, :], sm_raw[:, P * t : P * (t + 1)], ident_bf[:])
+        smT = keep.tile([P, 4, 64], F32)
+        nc.scalar.copy(out=smT[:], in_=smT_ps[:, :, 0:64])
 
         w1g = keep.tile([P, 2, CF, 4], BF16, align_bytes=64)
         w1_codes = keep.tile([P, 2, CF], U32, align_bytes=64)
@@ -111,20 +118,6 @@ def tile_mixtureconfounderprior_pa_kernel(
             scales=h_scales[:],
             in_=hg[:].rearrange("p g r t -> p (g r t)"),
         )
-        regroup(nc.vector.tensor_copy, w1g[:, 1, 0:W1_V], w1_raw[:, 1, :, 0:W1_V])
-        regroup(nc.scalar.copy, w1g[:, 1, W1_V:CF], w1_raw[:, 1, :, W1_V:CF])
-
-        smT_ps = pso.tile([P, 4, P], BF16, tag="o")
-        for t in range(4):
-            nc.tensor.transpose(smT_ps[:, t, :], sm_raw[:, P * t : P * (t + 1)], ident_bf[:])
-        smT = keep.tile([P, 4, P], F32)
-        nc.scalar.copy(out=smT[:], in_=smT_ps[:])
-
-        nc.vector.quantize_mx(
-            out=w1_codes[:, 0, :].bitcast(FP8X4),
-            scales=w1_scales[:, 0, :],
-            in_=w1g[:, 0].rearrange("p c t -> p (c t)"),
-        )
         cm1 = keep.tile([P, 4, NCODE], F32)
         nc.vector.tensor_tensor(
             out=cm1[:],
@@ -132,17 +125,41 @@ def tile_mixtureconfounderprior_pa_kernel(
             in1=smT[:, :, ROW_B1 : ROW_B1 + 1].to_broadcast([P, 4, NCODE]),
             op=ALU.add,
         )
+        cms = keep.tile([P, NCODE], F32)
+        nc.vector.tensor_reduce(
+            out=cms[:], in_=cm1[:].rearrange("p t c -> p c t"), axis=AX.X, op=ALU.add
+        )
         mc_ps = pso.tile([P, NCODE], F32, tag="o")
-        for t in range(4):
-            nc.tensor.matmul(
-                mc_ps[:], lhsT=ones[:], rhs=cm1[:, t, :], start=(t == 0), stop=(t == 3)
-            )
+        nc.tensor.matmul(mc_ps[:], lhsT=ones[:], rhs=cms[:], start=True, stop=True)
+        nc.vector.quantize_mx(
+            out=w1_codes[:, 0, :].bitcast(FP8X4),
+            scales=w1_scales[:, 0, :],
+            in_=w1g[:, 0].rearrange("p c t -> p (c t)"),
+        )
+        regroup(nc.vector.tensor_copy, w1g[:, 1, 0:W1_V], w1_raw[:, 1, :, 0:W1_V])
+        regroup(nc.scalar.copy, w1g[:, 1, W1_V:CF], w1_raw[:, 1, :, W1_V:CF])
         nc.vector.quantize_mx(
             out=w1_codes[:, 1, :].bitcast(FP8X4),
             scales=w1_scales[:, 1, :],
             in_=w1g[:, 1].rearrange("p c t -> p (c t)"),
         )
 
+        v_ps = pso.tile([P, NCODE], F32, tag="o")
+        hpT_ps = [
+            pso.tile([P, 2, TOK], F32, tag="o", name="hpT_ps0"),
+            pso.tile([P, 2, TOK], F32, tag="o", name="hpT_ps1"),
+        ]
+        for t in range(4):
+            for g in range(2):
+                nc.tensor.matmul_mx(
+                    out=hpT_ps[t // 2][:, t % 2, :],
+                    lhsT=w1_codes[:, g, P * t : P * (t + 1)].bitcast(FP8X4),
+                    lhsT_scale=w1_scales[:, g, P * t : P * (t + 1)],
+                    rhs=h_codes[:, TOK * g : TOK * (g + 1)].bitcast(FP8X4),
+                    rhs_scale=h_scales[:, TOK * g : TOK * (g + 1)],
+                    start=(g == 0),
+                    stop=(g == 1),
+                )
         hp_ps = pso.tile([P, CF], F32, tag="o")
         for g in range(2):
             nc.tensor.matmul_mx(
@@ -154,21 +171,6 @@ def tile_mixtureconfounderprior_pa_kernel(
                 start=(g == 0),
                 stop=(g == 1),
             )
-        hpT_ps = pso.tile([P, 4, TOK], F32, tag="o")
-        for t in range(4):
-            for g in range(2):
-                nc.tensor.matmul_mx(
-                    out=hpT_ps[:, t, :],
-                    lhsT=w1_codes[:, g, P * t : P * (t + 1)].bitcast(FP8X4),
-                    lhsT_scale=w1_scales[:, g, P * t : P * (t + 1)],
-                    rhs=h_codes[:, TOK * g : TOK * (g + 1)].bitcast(FP8X4),
-                    rhs_scale=h_scales[:, TOK * g : TOK * (g + 1)],
-                    start=(g == 0),
-                    stop=(g == 1),
-                )
-        hpT = keep.tile([P, 4, TOK], F32)
-        nc.scalar.copy(out=hpT[:], in_=hpT_ps[:])
-
         c_sb = keep.tile([P, 4, NCODE], F32)
         nc.vector.tensor_tensor(
             out=c_sb[:],
@@ -176,51 +178,63 @@ def tile_mixtureconfounderprior_pa_kernel(
             in1=mc_ps[:].unsqueeze(1).to_broadcast([P, 4, NCODE]),
             op=ALU.subtract,
         )
-        csq = keep.tile([P, 4, NCODE], F32)
-        nc.vector.tensor_tensor(out=csq[:], in0=c_sb[:], in1=c_sb[:], op=ALU.mult)
         c2 = keep.tile([P, 4, NCODE], F32)
         nc.vector.tensor_scalar_mul(out=c2[:], in0=c_sb[:], scalar1=2.0 / CF)
-        v_ps = pso.tile([P, NCODE], F32, tag="o")
+        csq = keep.tile([P, 4, NCODE], F32)
+        nc.vector.tensor_tensor(out=csq[:], in0=c_sb[:], in1=c_sb[:], op=ALU.mult)
+        cvs = keep.tile([P, NCODE], F32)
+        nc.vector.tensor_reduce(
+            out=cvs[:], in_=csq[:].rearrange("p t c -> p c t"), axis=AX.X, op=ALU.add
+        )
+        hpT0 = keep.tile([P, 2, TOK], F32)
+        nc.scalar.copy(out=hpT0[:], in_=hpT_ps[0][:])
+        hpT1 = keep.tile([P, 2, TOK], F32)
+        nc.vector.tensor_copy(out=hpT1[:], in_=hpT_ps[1][:])
+        hpT = [hpT0, hpT1]
+        nc.tensor.matmul(v_ps[:], lhsT=ones[:], rhs=cvs[:], start=True, stop=False)
         for t in range(4):
-            nc.tensor.matmul(v_ps[:], lhsT=ones[:], rhs=csq[:, t, :], start=(t == 0), stop=False)
+            nc.tensor.matmul(
+                v_ps[:], lhsT=hpT[t // 2][:, t % 2, :], rhs=c2[:, t, :], start=False, stop=(t == 3)
+            )
 
         st = keep.tile([P, 6], F32)
         nc.vector.bn_stats(out=st[:], in_=hp_ps[:])
         mv = keep.tile([P, 2], F32)
         nc.vector.bn_aggr(out=mv[:], in_=st[:])
+        vhe = keep.tile([P, 1], F32)
+        nc.vector.tensor_scalar_add(out=vhe[:], in0=mv[:, 1:2], scalar1=LN_EPS)
         hpc = keep.tile([P, CF], F32)
         nc.vector.tensor_scalar(
             out=hpc[:], in0=hp_ps[:], scalar1=mv[:, 0:1], scalar2=None, op0=ALU.subtract
         )
-        for t in range(4):
-            nc.tensor.matmul(v_ps[:], lhsT=hpT[:, t, :], rhs=c2[:, t, :], start=False, stop=(t == 3))
         aT_ps = pso.tile([P, 4, TOK], F32, tag="o")
         for t in range(4):
             nc.tensor.transpose(aT_ps[:, t, :], hpc[:, P * t : P * (t + 1)], ident[:])
-        vhe = keep.tile([P, 1], F32)
-        nc.vector.tensor_scalar_add(out=vhe[:], in0=mv[:, 1:2], scalar1=LN_EPS)
         std = keep.tile([P, NCODE], F32)
         nc.scalar.activation(out=std[:], in_=v_ps[:], func=ACT.Sqrt, bias=vhe[:, 0:1])
+        nc.scalar.activation(out=warm[:], in_=eps[:], func=ACT.Tanh)
+
+        w2g = keep.tile([P, CF, 4], BF16, align_bytes=64)
+        nc.gpsimd.tensor_scalar(
+            out=w2g[:],
+            in0=w2_raw[:].rearrange("p t c -> p c t"),
+            scalar1=1.0,
+            scalar2=0.0,
+            op0=ALU.mult,
+            op1=ALU.add,
+        )
+        w2_codes = keep.tile([P, CF], U32, align_bytes=64)
+        w2_scales = keep.tile([P, CF], U8, align_bytes=64)
+        nc.vector.quantize_mx(
+            out=w2_codes[:].bitcast(FP8X4),
+            scales=w2_scales[:],
+            in_=w2g[:].rearrange("p c t -> p (c t)"),
+        )
         r_sb = keep.tile([P, NCODE], F32)
         nc.vector.reciprocal(out=r_sb[:], in_=std[:])
         a_sb = keep.tile([P, 4, TOK], F32)
         nc.vector.tensor_copy(out=a_sb[:], in_=aT_ps[:])
-        nc.scalar.activation(out=warm[:], in_=eps[:], func=ACT.Tanh)
-
-        b2_ps = pso.tile([P, CF], F32, tag="o")
-        nc.tensor.matmul(
-            b2_ps[:],
-            lhsT=ident_bf[:, ROW_B2 : ROW_B2 + 1].to_broadcast([P, P]),
-            rhs=sm_raw[:],
-            start=True,
-            stop=True,
-        )
         b2_bc = keep.tile([P, CF], F32)
-        nc.scalar.copy(out=b2_bc[:], in_=b2_ps[:])
-        w2g = keep.tile([P, CF, 4], BF16, align_bytes=64)
-        regroup(nc.scalar.copy, w2g[:], w2_raw[:])
-        w2_codes = keep.tile([P, CF], U32, align_bytes=64)
-        w2_scales = keep.tile([P, CF], U8, align_bytes=64)
 
         tiles = {}
 
@@ -235,12 +249,8 @@ def tile_mixtureconfounderprior_pa_kernel(
                         r_ps = psr.tile([P, CG, TOK], F32, tag="r", name="r_ps")
                         tiles[("rt", rd)] = r_ps
                     tiles[("r", rd, cl)] = tiles[("rt", rd)][:, cl, :]
-                nc.tensor.matmul(
-                    tiles[("r", rd, cl)],
-                    lhsT=r_sb[:, code : code + 1].to_broadcast([P, P]),
-                    rhs=ident[:],
-                    start=True,
-                    stop=True,
+                nc.tensor.transpose(
+                    tiles[("r", rd, cl)], r_sb[:, code : code + 1].to_broadcast([P, P]), ident[:]
                 )
 
         def normalise(rd):
@@ -263,7 +273,7 @@ def tile_mixtureconfounderprior_pa_kernel(
             m = work.tile([P, 4, W], BF16, name="m")
             tiles[("m", rd)] = m
             for t in range(4):
-                if GB_ENG[t] == "s":
+                if GB_ENG[rd][t] == "s":
                     nc.scalar.activation(
                         out=m[:, t, :],
                         in_=z[:, t].rearrange("p c r -> p (c r)"),
@@ -285,10 +295,11 @@ def tile_mixtureconfounderprior_pa_kernel(
             m = tiles[("m", rd)]
             mg = work.tile([P, W, 4], BF16, align_bytes=64, name="mg")
             tiles[("mg", rd)] = mg
-            if RG_V > 0:
-                regroup(nc.vector.tensor_copy, mg[:, 0:RG_V], m[:, :, 0:RG_V])
-            if RG_V < W:
-                regroup(nc.scalar.copy, mg[:, RG_V:W], m[:, :, RG_V:W])
+            rv = RG_V[rd]
+            if rv > 0:
+                regroup(nc.vector.tensor_copy, mg[:, 0:rv], m[:, :, 0:rv])
+            if rv < W:
+                regroup(nc.scalar.copy, mg[:, rv:W], m[:, :, rv:W])
 
         def quantise_mu(rd):
             mg = tiles[("mg", rd)]
@@ -334,7 +345,7 @@ def tile_mixtureconfounderprior_pa_kernel(
 
         def normalise_part(rd, cls):
             if cls[0] == 0:
-                z_new = work.tile([P, 4, CG, TOK], F32, name="z")
+                z_new = zpool.tile([P, 4, CG, TOK], F32, name="z")
                 tiles[("z", rd)] = z_new
             z = tiles[("z", rd)]
             for cl in cls:
@@ -364,33 +375,40 @@ def tile_mixtureconfounderprior_pa_kernel(
             for cl in cls:
                 nc.scalar.activation(out=res[:, cl, :], in_=res[:, cl, :], func=ACT.Tanh)
 
-        bcast_r(0)
-        bcast_r(1)
-        normalise_part(0, [0, 1, 2, 3])
-        gain_bias(0)
-        normalise_part(1, [0, 1, 2, 3])
-        nc.vector.quantize_mx(
-            out=w2_codes[:].bitcast(FP8X4),
-            scales=w2_scales[:],
-            in_=w2g[:].rearrange("p c t -> p (c t)"),
-        )
+        def load_b2():
+            b2_ps = pso.tile([P, CF], F32, tag="o", name="b2_ps")
+            nc.tensor.matmul(
+                b2_ps[:],
+                lhsT=ident_bf[:, ROW_B2 : ROW_B2 + 1].to_broadcast([P, P]),
+                rhs=sm_raw[:],
+                start=True,
+                stop=True,
+            )
+            nc.scalar.copy(out=b2_bc[:], in_=b2_ps[:])
+
+        for rd in range(LEAD):
+            bcast_r(rd)
+        for rd in range(LEAD):
+            normalise_part(rd, [0, 1, 2, 3])
+            gain_bias(rd)
+            if rd == 0:
+                load_b2()
         for rd in range(ROUNDS):
-            more = rd + 2 < ROUNDS
+            more = rd + LEAD < ROUNDS
             if more:
-                bcast_r(rd + 2)
+                bcast_r(rd + LEAD)
             regroup_mu(rd)
-            if rd + 1 < ROUNDS:
-                gain_bias(rd + 1)
             if rd > 0:
                 add_b2(rd - 1, [0, 1, 2, 3])
                 tanh(rd - 1, [0, 1, 2, 3])
                 store(rd - 1, 0, CG)
             if more:
-                normalise_part(rd + 2, [0])
+                normalise_part(rd + LEAD, [0])
             quantise_mu(rd)
             second_mm(rd)
             if more:
-                normalise_part(rd + 2, [1,2,3])
+                normalise_part(rd + LEAD, [1, 2, 3])
+                gain_bias(rd + LEAD)
         last = ROUNDS - 1
         add_b2(last, [0, 1])
         tanh(last, [0, 1])

@@ -67,6 +67,8 @@ def tile_mixtureconfounderprior_pa_kernel(
                     "(u p e) c -> p u e c", u=2, e=2
                 ),
             )
+        w2_raw = keep.tile([P, 4, CF], BF16)
+        nc.sync.dma_start(out=w2_raw[:], in_=mu_w2.rearrange("(t p) n -> p t n", p=P))
         sm_raw = keep.tile([P, CF], BF16)
         nc.scalar.dma_start(out=sm_raw[0:NCODE, :], in_=code_mu)
         nc.scalar.dma_start(out=sm_raw[ROW_B1 : ROW_B1 + 8, :], in_=mu_b1.partition_broadcast(8))
@@ -79,8 +81,6 @@ def tile_mixtureconfounderprior_pa_kernel(
         make_identity(nc, ident[:])
         ident_bf = keep.tile([P, P], BF16)
         make_identity(nc, ident_bf[:])
-        w2_raw = keep.tile([P, 4, CF], BF16)
-        nc.gpsimd.dma_start(out=w2_raw[:], in_=mu_w2.rearrange("(t p) n -> p t n", p=P))
         ones = keep.tile([P, P], F32)
         nc.vector.memset(ones[:], 1.0 / CF)
         eps = keep.tile([P, 1], F32)
@@ -186,16 +186,14 @@ def tile_mixtureconfounderprior_pa_kernel(
         nc.vector.tensor_reduce(
             out=cvs[:], in_=csq[:].rearrange("p t c -> p c t"), axis=AX.X, op=ALU.add
         )
-        hpT0 = keep.tile([P, 2, TOK], F32)
-        nc.scalar.copy(out=hpT0[:], in_=hpT_ps[0][:])
-        hpT1 = keep.tile([P, 2, TOK], F32)
-        nc.vector.tensor_copy(out=hpT1[:], in_=hpT_ps[1][:])
-        hpT = [hpT0, hpT1]
+        w2g = keep.tile([P, CF, 4], BF16, align_bytes=64)
+        regroup(nc.scalar.copy, w2g[:], w2_raw[:])
+        hpT = keep.tile([P, 4, TOK], F32)
+        nc.vector.tensor_copy(out=hpT[:, 0:2, :], in_=hpT_ps[0][:])
+        nc.vector.tensor_copy(out=hpT[:, 2:4, :], in_=hpT_ps[1][:])
         nc.tensor.matmul(v_ps[:], lhsT=ones[:], rhs=cvs[:], start=True, stop=False)
         for t in range(4):
-            nc.tensor.matmul(
-                v_ps[:], lhsT=hpT[t // 2][:, t % 2, :], rhs=c2[:, t, :], start=False, stop=(t == 3)
-            )
+            nc.tensor.matmul(v_ps[:], lhsT=hpT[:, t, :], rhs=c2[:, t, :], start=False, stop=(t == 3))
 
         st = keep.tile([P, 6], F32)
         nc.vector.bn_stats(out=st[:], in_=hp_ps[:])
@@ -203,26 +201,11 @@ def tile_mixtureconfounderprior_pa_kernel(
         nc.vector.bn_aggr(out=mv[:], in_=st[:])
         vhe = keep.tile([P, 1], F32)
         nc.vector.tensor_scalar_add(out=vhe[:], in0=mv[:, 1:2], scalar1=LN_EPS)
-        hpc = keep.tile([P, CF], F32)
-        nc.vector.tensor_scalar(
-            out=hpc[:], in0=hp_ps[:], scalar1=mv[:, 0:1], scalar2=None, op0=ALU.subtract
-        )
-        aT_ps = pso.tile([P, 4, TOK], F32, tag="o")
-        for t in range(4):
-            nc.tensor.transpose(aT_ps[:, t, :], hpc[:, P * t : P * (t + 1)], ident[:])
+        mh_ps = pso.tile([P, TOK], F32, tag="o")
+        nc.tensor.transpose(mh_ps[:], mv[:, 0:1].to_broadcast([P, P]), ident[:])
         std = keep.tile([P, NCODE], F32)
         nc.scalar.activation(out=std[:], in_=v_ps[:], func=ACT.Sqrt, bias=vhe[:, 0:1])
         nc.scalar.activation(out=warm[:], in_=eps[:], func=ACT.Tanh)
-
-        w2g = keep.tile([P, CF, 4], BF16, align_bytes=64)
-        nc.gpsimd.tensor_scalar(
-            out=w2g[:],
-            in0=w2_raw[:].rearrange("p t c -> p c t"),
-            scalar1=1.0,
-            scalar2=0.0,
-            op0=ALU.mult,
-            op1=ALU.add,
-        )
         w2_codes = keep.tile([P, CF], U32, align_bytes=64)
         w2_scales = keep.tile([P, CF], U8, align_bytes=64)
         nc.vector.quantize_mx(
@@ -233,7 +216,12 @@ def tile_mixtureconfounderprior_pa_kernel(
         r_sb = keep.tile([P, NCODE], F32)
         nc.vector.reciprocal(out=r_sb[:], in_=std[:])
         a_sb = keep.tile([P, 4, TOK], F32)
-        nc.vector.tensor_copy(out=a_sb[:], in_=aT_ps[:])
+        nc.vector.tensor_tensor(
+            out=a_sb[:],
+            in0=hpT[:],
+            in1=mh_ps[:].unsqueeze(1).to_broadcast([P, 4, TOK]),
+            op=ALU.subtract,
+        )
         b2_bc = keep.tile([P, CF], F32)
 
         tiles = {}

@@ -30,8 +30,8 @@ ROW_B = 48
 ROW_B2 = 56
 
 GB_ENG = [["s","s","g","g"],["g","g","g","g"],["g","g","g","g"],["g","g","g","g"],["g","g","g","g"],["g","g","g","g"],["g","g","g","g"],["g","g","g","g"]]
-RG_V = [0,0,0,0,0,256,256,256]
-LEAD = 3
+RG_V = [0,0,0,0,0,0,0,0]
+LEAD = 2
 W1_V = 352
 
 
@@ -52,7 +52,7 @@ def tile_mixtureconfounderprior_pa_kernel(
     with ExitStack() as ctx:
         keep = ctx.enter_context(tc.tile_pool(name="keep", bufs=1))
         work = ctx.enter_context(tc.tile_pool(name="work", bufs=3))
-        zpool = ctx.enter_context(tc.tile_pool(name="zpool", bufs=4))
+        zpool = ctx.enter_context(tc.tile_pool(name="zpool", bufs=3))
         psr = ctx.enter_context(tc.psum_pool(name="psr", bufs=2))
         pso = ctx.enter_context(tc.psum_pool(name="pso", bufs=6))
         ctx.enter_context(tc.manual_schedule())
@@ -374,7 +374,7 @@ def tile_mixtureconfounderprior_pa_kernel(
             )
             nc.scalar.copy(out=b2_bc[:], in_=b2_ps[:])
 
-        for rd in range(LEAD):
+        for rd in range(LEAD + 1):
             bcast_r(rd)
         for rd in range(LEAD):
             normalise_part(rd, [0, 1, 2, 3])
@@ -383,19 +383,21 @@ def tile_mixtureconfounderprior_pa_kernel(
                 load_b2()
         for rd in range(ROUNDS):
             more = rd + LEAD < ROUNDS
-            if more:
-                bcast_r(rd + LEAD)
+            if rd + LEAD + 1 < ROUNDS:
+                bcast_r(rd + LEAD + 1)
             regroup_mu(rd)
+            if more:
+                normalise_part(rd + LEAD, [0])
             if rd > 0:
                 add_b2(rd - 1, [0, 1, 2, 3])
                 tanh(rd - 1, [0, 1, 2, 3])
                 store(rd - 1, 0, CG)
             if more:
-                normalise_part(rd + LEAD, [0])
+                normalise_part(rd + LEAD, [1, 2])
             quantise_mu(rd)
             second_mm(rd)
             if more:
-                normalise_part(rd + LEAD, [1, 2, 3])
+                normalise_part(rd + LEAD, [3])
                 gain_bias(rd + LEAD)
         last = ROUNDS - 1
         add_b2(last, [0, 1])

@@ -21,6 +21,7 @@ LN_EPS = 1e-5
 CG = 4
 ROUNDS = NCODE // CG
 W = CG * TOK
+LEAD = 2
 
 FLOPS = 2 * TOK * D_IN * CF + 2 * TOK * NCODE * CF * CF
 
@@ -28,10 +29,6 @@ ROW_B1 = 32
 ROW_G = 40
 ROW_B = 48
 ROW_B2 = 56
-
-GB_ENG = [["s","s","g","g"],["g","g","g","g"],["g","g","g","g"],["g","g","g","g"],["g","g","g","g"],["g","g","g","g"],["g","g","g","g"],["g","g","g","g"]]
-RG_V = [0,0,0,0,0,0,0,0]
-LEAD = 2
 W1_V = 352
 
 
@@ -52,7 +49,6 @@ def tile_mixtureconfounderprior_pa_kernel(
     with ExitStack() as ctx:
         keep = ctx.enter_context(tc.tile_pool(name="keep", bufs=1))
         work = ctx.enter_context(tc.tile_pool(name="work", bufs=3))
-        zpool = ctx.enter_context(tc.tile_pool(name="zpool", bufs=3))
         psr = ctx.enter_context(tc.psum_pool(name="psr", bufs=2))
         pso = ctx.enter_context(tc.psum_pool(name="pso", bufs=6))
         ctx.enter_context(tc.manual_schedule())
@@ -144,15 +140,12 @@ def tile_mixtureconfounderprior_pa_kernel(
             in_=w1g[:, 1].rearrange("p c t -> p (c t)"),
         )
 
-        v_ps = pso.tile([P, NCODE], F32, tag="o")
-        hpT_ps = [
-            pso.tile([P, 2, TOK], F32, tag="o", name="hpT_ps0"),
-            pso.tile([P, 2, TOK], F32, tag="o", name="hpT_ps1"),
-        ]
-        for t in range(4):
-            for g in range(2):
+        hpT_ps = [pso.tile([P, TOK], F32, tag="o", name="hpT_ps%d" % t) for t in range(4)]
+        hp_ps = pso.tile([P, CF], F32, tag="o")
+        for g in range(2):
+            for t in range(4):
                 nc.tensor.matmul_mx(
-                    out=hpT_ps[t // 2][:, t % 2, :],
+                    out=hpT_ps[t][:],
                     lhsT=w1_codes[:, g, P * t : P * (t + 1)].bitcast(FP8X4),
                     lhsT_scale=w1_scales[:, g, P * t : P * (t + 1)],
                     rhs=h_codes[:, TOK * g : TOK * (g + 1)].bitcast(FP8X4),
@@ -160,8 +153,6 @@ def tile_mixtureconfounderprior_pa_kernel(
                     start=(g == 0),
                     stop=(g == 1),
                 )
-        hp_ps = pso.tile([P, CF], F32, tag="o")
-        for g in range(2):
             nc.tensor.matmul_mx(
                 out=hp_ps[:],
                 lhsT=h_codes[:, TOK * g : TOK * (g + 1)].bitcast(FP8X4),
@@ -187,13 +178,18 @@ def tile_mixtureconfounderprior_pa_kernel(
             out=cvs[:], in_=csq[:].rearrange("p t c -> p c t"), axis=AX.X, op=ALU.add
         )
         w2g = keep.tile([P, CF, 4], BF16, align_bytes=64)
-        regroup(nc.scalar.copy, w2g[:], w2_raw[:])
-        hpT = keep.tile([P, 4, TOK], F32)
-        nc.vector.tensor_copy(out=hpT[:, 0:2, :], in_=hpT_ps[0][:])
-        nc.vector.tensor_copy(out=hpT[:, 2:4, :], in_=hpT_ps[1][:])
+        regroup(nc.scalar.copy, w2g[:, 0 : CF // 2], w2_raw[:, :, 0 : CF // 2])
+        hpT_v = keep.tile([P, 2, TOK], F32)
+        hpT_s = keep.tile([P, 2, TOK], F32)
+        for i in range(2):
+            nc.vector.tensor_copy(out=hpT_v[:, i, :], in_=hpT_ps[i][:])
+            nc.scalar.copy(out=hpT_s[:, i, :], in_=hpT_ps[2 + i][:])
+        hpT = [hpT_v[:, 0, :], hpT_v[:, 1, :], hpT_s[:, 0, :], hpT_s[:, 1, :]]
+        regroup(nc.scalar.copy, w2g[:, CF // 2 : CF], w2_raw[:, :, CF // 2 : CF])
+        v_ps = pso.tile([P, NCODE], F32, tag="o")
         nc.tensor.matmul(v_ps[:], lhsT=ones[:], rhs=cvs[:], start=True, stop=False)
         for t in range(4):
-            nc.tensor.matmul(v_ps[:], lhsT=hpT[:, t, :], rhs=c2[:, t, :], start=False, stop=(t == 3))
+            nc.tensor.matmul(v_ps[:], lhsT=hpT[t], rhs=c2[:, t, :], start=False, stop=(t == 3))
 
         st = keep.tile([P, 6], F32)
         nc.vector.bn_stats(out=st[:], in_=hp_ps[:])
@@ -217,9 +213,15 @@ def tile_mixtureconfounderprior_pa_kernel(
         nc.vector.reciprocal(out=r_sb[:], in_=std[:])
         a_sb = keep.tile([P, 4, TOK], F32)
         nc.vector.tensor_tensor(
-            out=a_sb[:],
-            in0=hpT[:],
-            in1=mh_ps[:].unsqueeze(1).to_broadcast([P, 4, TOK]),
+            out=a_sb[:, 0:2, :],
+            in0=hpT_v[:],
+            in1=mh_ps[:].unsqueeze(1).to_broadcast([P, 2, TOK]),
+            op=ALU.subtract,
+        )
+        nc.vector.tensor_tensor(
+            out=a_sb[:, 2:4, :],
+            in0=hpT_s[:],
+            in1=mh_ps[:].unsqueeze(1).to_broadcast([P, 2, TOK]),
             op=ALU.subtract,
         )
         b2_bc = keep.tile([P, CF], F32)
@@ -241,10 +243,23 @@ def tile_mixtureconfounderprior_pa_kernel(
                     tiles[("r", rd, cl)], r_sb[:, code : code + 1].to_broadcast([P, P]), ident[:]
                 )
 
-        def normalise(rd):
-            z = work.tile([P, 4, CG, TOK], F32, name="z")
-            tiles[("z", rd)] = z
-            for cl in range(CG):
+        def load_b2():
+            b2_ps = pso.tile([P, CF], F32, tag="o", name="b2_ps")
+            nc.tensor.matmul(
+                b2_ps[:],
+                lhsT=ident_bf[:, ROW_B2 : ROW_B2 + 1].to_broadcast([P, P]),
+                rhs=sm_raw[:],
+                start=True,
+                stop=True,
+            )
+            nc.scalar.copy(out=b2_bc[:], in_=b2_ps[:])
+
+        def normalise(rd, cls):
+            if cls[0] == 0:
+                z_new = work.tile([P, 4, CG, TOK], F32, name="z")
+                tiles[("z", rd)] = z_new
+            z = tiles[("z", rd)]
+            for cl in cls:
                 code = CG * rd + cl
                 for t in range(4):
                     nc.vector.scalar_tensor_tensor(
@@ -256,12 +271,14 @@ def tile_mixtureconfounderprior_pa_kernel(
                         op1=ALU.mult,
                     )
 
-        def gain_bias(rd):
+        def gain_bias(rd, planes, eng):
             z = tiles[("z", rd)]
-            m = work.tile([P, 4, W], BF16, name="m")
-            tiles[("m", rd)] = m
-            for t in range(4):
-                if GB_ENG[rd][t] == "s":
+            if ("m", rd) not in tiles:
+                m_new = work.tile([P, 4, W], BF16, name="m")
+                tiles[("m", rd)] = m_new
+            m = tiles[("m", rd)]
+            for t in planes:
+                if eng == "s":
                     nc.scalar.activation(
                         out=m[:, t, :],
                         in_=z[:, t].rearrange("p c r -> p (c r)"),
@@ -270,7 +287,8 @@ def tile_mixtureconfounderprior_pa_kernel(
                         bias=smT[:, t, ROW_B : ROW_B + 1],
                     )
                 else:
-                    nc.gpsimd.tensor_scalar(
+                    engine = nc.gpsimd if eng == "g" else nc.vector
+                    engine.tensor_scalar(
                         out=m[:, t, :],
                         in0=z[:, t].rearrange("p c r -> p (c r)"),
                         scalar1=smT[:, t, ROW_G : ROW_G + 1],
@@ -279,11 +297,10 @@ def tile_mixtureconfounderprior_pa_kernel(
                         op1=ALU.add,
                     )
 
-        def regroup_mu(rd):
+        def regroup_mu(rd, rv):
             m = tiles[("m", rd)]
             mg = work.tile([P, W, 4], BF16, align_bytes=64, name="mg")
             tiles[("mg", rd)] = mg
-            rv = RG_V[rd]
             if rv > 0:
                 regroup(nc.vector.tensor_copy, mg[:, 0:rv], m[:, :, 0:rv])
             if rv < W:
@@ -315,97 +332,59 @@ def tile_mixtureconfounderprior_pa_kernel(
                     stop=True,
                 )
 
-        def finish(rd, cls):
-            if cls[0] == 0:
+        def finish(rd, cls, lo=0, hi=CF):
+            if ("res", rd) not in tiles:
                 res_new = work.tile([P, CG, CF], F32, name="res")
                 tiles[("res", rd)] = res_new
             res = tiles[("res", rd)]
             for cl in cls:
                 nc.vector.tensor_tensor(
-                    out=res[:, cl, :], in0=tiles[("o", rd, cl)][:], in1=b2_bc[:], op=ALU.add
+                    out=res[:, cl, lo:hi],
+                    in0=tiles[("o", rd, cl)][:, lo:hi],
+                    in1=b2_bc[:, lo:hi],
+                    op=ALU.add,
                 )
             for cl in cls:
-                nc.scalar.activation(out=res[:, cl, :], in_=res[:, cl, :], func=ACT.Tanh)
-
-        def store(rd, lo, hi):
-            res = tiles[("res", rd)]
-            nc.sync.dma_start(out=out3[:, CG * rd + lo : CG * rd + hi, :], in_=res[:, lo:hi, :])
-
-        def normalise_part(rd, cls):
-            if cls[0] == 0:
-                z_new = zpool.tile([P, 4, CG, TOK], F32, name="z")
-                tiles[("z", rd)] = z_new
-            z = tiles[("z", rd)]
-            for cl in cls:
-                code = CG * rd + cl
-                for t in range(4):
-                    nc.vector.scalar_tensor_tensor(
-                        out=z[:, t, cl, :],
-                        in0=a_sb[:, t, :],
-                        scalar=c_sb[:, t, code : code + 1],
-                        in1=tiles[("r", rd, cl)],
-                        op0=ALU.add,
-                        op1=ALU.mult,
-                    )
-
-        def add_b2(rd, cls):
-            if cls[0] == 0:
-                res_new = work.tile([P, CG, CF], F32, name="res")
-                tiles[("res", rd)] = res_new
-            res = tiles[("res", rd)]
-            for cl in cls:
-                nc.vector.tensor_tensor(
-                    out=res[:, cl, :], in0=tiles[("o", rd, cl)][:], in1=b2_bc[:], op=ALU.add
-                )
-
-        def tanh(rd, cls):
-            res = tiles[("res", rd)]
-            for cl in cls:
-                nc.scalar.activation(out=res[:, cl, :], in_=res[:, cl, :], func=ACT.Tanh)
-
-        def load_b2():
-            b2_ps = pso.tile([P, CF], F32, tag="o", name="b2_ps")
-            nc.tensor.matmul(
-                b2_ps[:],
-                lhsT=ident_bf[:, ROW_B2 : ROW_B2 + 1].to_broadcast([P, P]),
-                rhs=sm_raw[:],
-                start=True,
-                stop=True,
+                nc.scalar.activation(out=res[:, cl, lo:hi], in_=res[:, cl, lo:hi], func=ACT.Tanh)
+            c0 = CG * rd + cls[0]
+            c1 = CG * rd + cls[-1] + 1
+            nc.sync.dma_start(
+                out=out3[:, c0:c1, lo:hi], in_=res[:, cls[0] : cls[-1] + 1, lo:hi]
             )
-            nc.scalar.copy(out=b2_bc[:], in_=b2_ps[:])
 
         for rd in range(LEAD + 1):
             bcast_r(rd)
-        for rd in range(LEAD):
-            normalise_part(rd, [0, 1, 2, 3])
-            gain_bias(rd)
-            if rd == 0:
-                load_b2()
+        normalise(0, [0, 1, 2, 3])
+        gain_bias(0, [0, 1], "s")
+        gain_bias(0, [2, 3], "g")
+        load_b2()
+        normalise(1, [0, 1, 2, 3])
+        gain_bias(1, [2, 3], "g")
         for rd in range(ROUNDS):
-            more = rd + LEAD < ROUNDS
-            if rd + LEAD + 1 < ROUNDS:
-                bcast_r(rd + LEAD + 1)
-            regroup_mu(rd)
+            nxt = rd + LEAD
+            more = nxt < ROUNDS
+            if nxt + 1 < ROUNDS:
+                bcast_r(nxt + 1)
+            regroup_mu(rd, 256 if rd == ROUNDS - 1 else 0)
+            if rd == 0:
+                gain_bias(1, [0, 1], "s")
             if more:
-                normalise_part(rd + LEAD, [0])
+                normalise(nxt, [0])
             if rd > 0:
-                add_b2(rd - 1, [0, 1, 2, 3])
-                tanh(rd - 1, [0, 1, 2, 3])
-                store(rd - 1, 0, CG)
+                finish(rd - 1, [0, 1, 2, 3])
             if more:
-                normalise_part(rd + LEAD, [1, 2])
+                normalise(nxt, [1, 2])
             quantise_mu(rd)
             second_mm(rd)
             if more:
-                normalise_part(rd + LEAD, [3])
-                gain_bias(rd + LEAD)
+                normalise(nxt, [3])
+                if nxt == ROUNDS - 1:
+                    gain_bias(nxt, [0, 1], "v")
+                    gain_bias(nxt, [2, 3], "g")
+                else:
+                    gain_bias(nxt, [0, 1, 2, 3], "g")
         last = ROUNDS - 1
-        add_b2(last, [0, 1])
-        tanh(last, [0, 1])
-        store(last, 0, 2)
-        add_b2(last, [2])
-        tanh(last, [2])
-        store(last, 2, 3)
-        add_b2(last, [3])
-        tanh(last, [3])
-        store(last, 3, 4)
+        finish(last, [0, 1])
+        finish(last, [2])
+        finish(last, [3], 0, CF // 2)
+        finish(last, [3], CF // 2, CF)

@@ -162,6 +162,17 @@ def tile_mixtureconfounderprior_pa_kernel(
                 start=(g == 0),
                 stop=(g == 1),
             )
+            if g == 0:
+                b2_ps = psr.tile([P, CF], F32, tag="r")
+                nc.tensor.matmul(
+                    b2_ps[:],
+                    lhsT=ident_bf[:, ROW_B2 : ROW_B2 + 1].to_broadcast([P, P]),
+                    rhs=sm_raw[:],
+                    start=True,
+                    stop=True,
+                )
+                b2_bc = keep.tile([P, CF], F32)
+                nc.scalar.copy(out=b2_bc[:], in_=b2_ps[:])
         c_sb = keep.tile([P, 4, NCODE], F32)
         nc.vector.tensor_tensor(
             out=c_sb[:],
@@ -178,18 +189,14 @@ def tile_mixtureconfounderprior_pa_kernel(
             out=cvs[:], in_=csq[:].rearrange("p t c -> p c t"), axis=AX.X, op=ALU.add
         )
         w2g = keep.tile([P, CF, 4], BF16, align_bytes=64)
-        regroup(nc.scalar.copy, w2g[:, 0 : CF // 2], w2_raw[:, :, 0 : CF // 2])
-        hpT_v = keep.tile([P, 2, TOK], F32)
-        hpT_s = keep.tile([P, 2, TOK], F32)
-        for i in range(2):
-            nc.vector.tensor_copy(out=hpT_v[:, i, :], in_=hpT_ps[i][:])
-            nc.scalar.copy(out=hpT_s[:, i, :], in_=hpT_ps[2 + i][:])
-        hpT = [hpT_v[:, 0, :], hpT_v[:, 1, :], hpT_s[:, 0, :], hpT_s[:, 1, :]]
-        regroup(nc.scalar.copy, w2g[:, CF // 2 : CF], w2_raw[:, :, CF // 2 : CF])
+        regroup(nc.scalar.copy, w2g[:], w2_raw[:])
+        hpT_sb = keep.tile([P, 4, TOK], F32)
+        for t in range(4):
+            nc.vector.tensor_copy(out=hpT_sb[:, t, :], in_=hpT_ps[t][:])
         v_ps = pso.tile([P, NCODE], F32, tag="o")
         nc.tensor.matmul(v_ps[:], lhsT=ones[:], rhs=cvs[:], start=True, stop=False)
         for t in range(4):
-            nc.tensor.matmul(v_ps[:], lhsT=hpT[t], rhs=c2[:, t, :], start=False, stop=(t == 3))
+            nc.tensor.matmul(v_ps[:], lhsT=hpT_sb[:, t, :], rhs=c2[:, t, :], start=False, stop=(t == 3))
 
         st = keep.tile([P, 6], F32)
         nc.vector.bn_stats(out=st[:], in_=hp_ps[:])
@@ -213,18 +220,11 @@ def tile_mixtureconfounderprior_pa_kernel(
         nc.vector.reciprocal(out=r_sb[:], in_=std[:])
         a_sb = keep.tile([P, 4, TOK], F32)
         nc.vector.tensor_tensor(
-            out=a_sb[:, 0:2, :],
-            in0=hpT_v[:],
-            in1=mh_ps[:].unsqueeze(1).to_broadcast([P, 2, TOK]),
+            out=a_sb[:],
+            in0=hpT_sb[:],
+            in1=mh_ps[:].unsqueeze(1).to_broadcast([P, 4, TOK]),
             op=ALU.subtract,
         )
-        nc.vector.tensor_tensor(
-            out=a_sb[:, 2:4, :],
-            in0=hpT_s[:],
-            in1=mh_ps[:].unsqueeze(1).to_broadcast([P, 2, TOK]),
-            op=ALU.subtract,
-        )
-        b2_bc = keep.tile([P, CF], F32)
 
         tiles = {}
 
@@ -243,17 +243,6 @@ def tile_mixtureconfounderprior_pa_kernel(
                     tiles[("r", rd, cl)], r_sb[:, code : code + 1].to_broadcast([P, P]), ident[:]
                 )
 
-        def load_b2():
-            b2_ps = pso.tile([P, CF], F32, tag="o", name="b2_ps")
-            nc.tensor.matmul(
-                b2_ps[:],
-                lhsT=ident_bf[:, ROW_B2 : ROW_B2 + 1].to_broadcast([P, P]),
-                rhs=sm_raw[:],
-                start=True,
-                stop=True,
-            )
-            nc.scalar.copy(out=b2_bc[:], in_=b2_ps[:])
-
         def normalise(rd, cls):
             if cls[0] == 0:
                 z_new = work.tile([P, 4, CG, TOK], F32, name="z")
@@ -271,13 +260,13 @@ def tile_mixtureconfounderprior_pa_kernel(
                         op1=ALU.mult,
                     )
 
-        def gain_bias(rd, planes, eng):
+        def gain_bias(rd, chunks, eng):
             z = tiles[("z", rd)]
             if ("m", rd) not in tiles:
                 m_new = work.tile([P, 4, W], BF16, name="m")
                 tiles[("m", rd)] = m_new
             m = tiles[("m", rd)]
-            for t in planes:
+            for t in chunks:
                 if eng == "s":
                     nc.scalar.activation(
                         out=m[:, t, :],
@@ -297,14 +286,13 @@ def tile_mixtureconfounderprior_pa_kernel(
                         op1=ALU.add,
                     )
 
-        def regroup_mu(rd, rv):
+        def regroup_mu(rd, vector_rows):
             m = tiles[("m", rd)]
             mg = work.tile([P, W, 4], BF16, align_bytes=64, name="mg")
             tiles[("mg", rd)] = mg
-            if rv > 0:
-                regroup(nc.vector.tensor_copy, mg[:, 0:rv], m[:, :, 0:rv])
-            if rv < W:
-                regroup(nc.scalar.copy, mg[:, rv:W], m[:, :, rv:W])
+            if vector_rows > 0:
+                regroup(nc.vector.tensor_copy, mg[:, 0:vector_rows], m[:, :, 0:vector_rows])
+            regroup(nc.scalar.copy, mg[:, vector_rows:W], m[:, :, vector_rows:W])
 
         def quantise_mu(rd):
             mg = tiles[("mg", rd)]
@@ -357,7 +345,6 @@ def tile_mixtureconfounderprior_pa_kernel(
         normalise(0, [0, 1, 2, 3])
         gain_bias(0, [0, 1], "s")
         gain_bias(0, [2, 3], "g")
-        load_b2()
         normalise(1, [0, 1, 2, 3])
         gain_bias(1, [2, 3], "g")
         for rd in range(ROUNDS):
@@ -365,7 +352,7 @@ def tile_mixtureconfounderprior_pa_kernel(
             more = nxt < ROUNDS
             if nxt + 1 < ROUNDS:
                 bcast_r(nxt + 1)
-            regroup_mu(rd, 256 if rd == ROUNDS - 1 else 0)
+            regroup_mu(rd, W // 2 if rd == ROUNDS - 1 else 0)
             if rd == 0:
                 gain_bias(1, [0, 1], "s")
             if more:

from contextlib import ExitStack

from concourse import mybir
from concourse.masks import make_identity

F32 = mybir.dt.float32
BF16 = mybir.dt.bfloat16
U32 = mybir.dt.uint32
U8 = mybir.dt.uint8
FP8X4 = mybir.dt.float8_e4m3fn_x4
ALU = mybir.AluOpType
ACT = mybir.ActivationFunctionType
AX = mybir.AxisListType

P = 128
TOK = 128
D_IN = 1024
CF = 512
NCODE = 32
LN_EPS = 1e-5
CG = 4
ROUNDS = NCODE // CG
W = CG * TOK
LEAD = 2

FLOPS = 2 * TOK * D_IN * CF + 2 * TOK * NCODE * CF * CF

ROW_B1 = 32
ROW_G = 40
ROW_B = 48
ROW_B2 = 56
W1_V = 352


def regroup(eng_copy, dst, src):
    eng_copy(
        out=dst.rearrange("p (c i) t -> p c t i", i=4),
        in_=src.rearrange("p t (c i) -> p c t i", i=4),
    )


def tile_mixtureconfounderprior_pa_kernel(
    tc, h, mu_w1_h, code_mu, mu_b1, ln_g, ln_b, mu_w2, mu_b2, out
):
    nc = tc.nc
    h2 = h.rearrange("b t d -> (b t) d")
    out3 = out.rearrange("b t k n -> (b t) k n")

    with ExitStack() as ctx:
        keep = ctx.enter_context(tc.tile_pool(name="keep", bufs=1))
        work = ctx.enter_context(tc.tile_pool(name="work", bufs=3))
        psr = ctx.enter_context(tc.psum_pool(name="psr", bufs=2))
        pso = ctx.enter_context(tc.psum_pool(name="pso", bufs=6))
        ctx.enter_context(tc.manual_schedule())

        h_sb = keep.tile([P, D_IN], BF16)
        nc.sync.dma_start(out=h_sb[:], in_=h2)
        w1_raw = keep.tile([P, 2, 4, CF], BF16)
        for g in range(2):
            nc.sync.dma_start(
                out=w1_raw[:, g].rearrange("p (u e) c -> p u e c", u=2),
                in_=mu_w1_h[512 * g : 512 * (g + 1), :].rearrange(
                    "(u p e) c -> p u e c", u=2, e=2
                ),
            )
        w2_raw = keep.tile([P, 4, CF], BF16)
        nc.sync.dma_start(out=w2_raw[:], in_=mu_w2.rearrange("(t p) n -> p t n", p=P))
        sm_raw = keep.tile([P, CF], BF16)
        nc.scalar.dma_start(out=sm_raw[0:NCODE, :], in_=code_mu)
        nc.scalar.dma_start(out=sm_raw[ROW_B1 : ROW_B1 + 8, :], in_=mu_b1.partition_broadcast(8))
        nc.scalar.dma_start(out=sm_raw[ROW_G : ROW_G + 8, :], in_=ln_g.partition_broadcast(8))
        nc.scalar.dma_start(out=sm_raw[ROW_B : ROW_B + 8, :], in_=ln_b.partition_broadcast(8))
        nc.scalar.dma_start(out=sm_raw[ROW_B2 : ROW_B2 + 8, :], in_=mu_b2.partition_broadcast(8))
        nc.vector.memset(sm_raw[64:128, :].bitcast(F32), 0.0)

        ident = keep.tile([P, P], F32)
        make_identity(nc, ident[:])
        ident_bf = keep.tile([P, P], BF16)
        make_identity(nc, ident_bf[:])
        ones = keep.tile([P, P], F32)
        nc.vector.memset(ones[:], 1.0 / CF)
        eps = keep.tile([P, 1], F32)
        nc.vector.memset(eps[:], LN_EPS)
        warm = keep.tile([P, 1], F32)
        nc.scalar.activation(out=warm[:], in_=eps[:], func=ACT.Sqrt)

        h_w = h_sb[:].bitcast(F32)
        xt = pso.tile([P, 2, 2, P], F32, tag="o")
        for g in range(2):
            for u in range(2):
                nc.tensor.transpose(
                    xt[:, g, u, :], h_w[:, 256 * g + 128 * u : 256 * g + 128 * u + 128], ident[:]
                )
        hg = keep.tile([P, 2, TOK, 4], BF16, align_bytes=64)
        nc.vector.tensor_copy(
            out=hg[:].bitcast(F32), in_=xt[:].rearrange("p g u r -> p g r u")
        )
        smT_ps = pso.tile([P, 4, P], BF16, tag="o")
        for t in range(4):
            nc.tensor.transpose(smT_ps[:, t, :], sm_raw[:, P * t : P * (t + 1)], ident_bf[:])
        smT = keep.tile([P, 4, 64], F32)
        nc.scalar.copy(out=smT[:], in_=smT_ps[:, :, 0:64])

        w1g = keep.tile([P, 2, CF, 4], BF16, align_bytes=64)
        w1_codes = keep.tile([P, 2, CF], U32, align_bytes=64)
        w1_scales = keep.tile([P, 2, CF], U8, align_bytes=64)
        h_codes = keep.tile([P, 2 * TOK], U32, align_bytes=64)
        h_scales = keep.tile([P, 2 * TOK], U8, align_bytes=64)

        regroup(nc.vector.tensor_copy, w1g[:, 0, 0:W1_V], w1_raw[:, 0, :, 0:W1_V])
        regroup(nc.scalar.copy, w1g[:, 0, W1_V:CF], w1_raw[:, 0, :, W1_V:CF])
        nc.vector.quantize_mx(
            out=h_codes[:].bitcast(FP8X4),
            scales=h_scales[:],
            in_=hg[:].rearrange("p g r t -> p (g r t)"),
        )
        cm1 = keep.tile([P, 4, NCODE], F32)
        nc.vector.tensor_tensor(
            out=cm1[:],
            in0=smT[:, :, 0:NCODE],
            in1=smT[:, :, ROW_B1 : ROW_B1 + 1].to_broadcast([P, 4, NCODE]),
            op=ALU.add,
        )
        cms = keep.tile([P, NCODE], F32)
        nc.vector.tensor_reduce(
            out=cms[:], in_=cm1[:].rearrange("p t c -> p c t"), axis=AX.X, op=ALU.add
        )
        mc_ps = pso.tile([P, NCODE], F32, tag="o")
        nc.tensor.matmul(mc_ps[:], lhsT=ones[:], rhs=cms[:], start=True, stop=True)
        nc.vector.quantize_mx(
            out=w1_codes[:, 0, :].bitcast(FP8X4),
            scales=w1_scales[:, 0, :],
            in_=w1g[:, 0].rearrange("p c t -> p (c t)"),
        )
        regroup(nc.vector.tensor_copy, w1g[:, 1, 0:W1_V], w1_raw[:, 1, :, 0:W1_V])
        regroup(nc.scalar.copy, w1g[:, 1, W1_V:CF], w1_raw[:, 1, :, W1_V:CF])
        nc.vector.quantize_mx(
            out=w1_codes[:, 1, :].bitcast(FP8X4),
            scales=w1_scales[:, 1, :],
            in_=w1g[:, 1].rearrange("p c t -> p (c t)"),
        )

        hpT_ps = [pso.tile([P, TOK], F32, tag="o", name="hpT_ps%d" % t) for t in range(4)]
        hp_ps = pso.tile([P, CF], F32, tag="o")
        for g in range(2):
            for t in range(4):
                nc.tensor.matmul_mx(
                    out=hpT_ps[t][:],
                    lhsT=w1_codes[:, g, P * t : P * (t + 1)].bitcast(FP8X4),
                    lhsT_scale=w1_scales[:, g, P * t : P * (t + 1)],
                    rhs=h_codes[:, TOK * g : TOK * (g + 1)].bitcast(FP8X4),
                    rhs_scale=h_scales[:, TOK * g : TOK * (g + 1)],
                    start=(g == 0),
                    stop=(g == 1),
                )
            nc.tensor.matmul_mx(
                out=hp_ps[:],
                lhsT=h_codes[:, TOK * g : TOK * (g + 1)].bitcast(FP8X4),
                lhsT_scale=h_scales[:, TOK * g : TOK * (g + 1)],
                rhs=w1_codes[:, g, :].bitcast(FP8X4),
                rhs_scale=w1_scales[:, g, :],
                start=(g == 0),
                stop=(g == 1),
            )
            if g == 0:
                b2_ps = psr.tile([P, CF], F32, tag="r")
                nc.tensor.matmul(
                    b2_ps[:],
                    lhsT=ident_bf[:, ROW_B2 : ROW_B2 + 1].to_broadcast([P, P]),
                    rhs=sm_raw[:],
                    start=True,
                    stop=True,
                )
                b2_bc = keep.tile([P, CF], F32)
                nc.scalar.copy(out=b2_bc[:], in_=b2_ps[:])
        c_sb = keep.tile([P, 4, NCODE], F32)
        nc.vector.tensor_tensor(
            out=c_sb[:],
            in0=cm1[:],
            in1=mc_ps[:].unsqueeze(1).to_broadcast([P, 4, NCODE]),
            op=ALU.subtract,
        )
        c2 = keep.tile([P, 4, NCODE], F32)
        nc.vector.tensor_scalar_mul(out=c2[:], in0=c_sb[:], scalar1=2.0 / CF)
        csq = keep.tile([P, 4, NCODE], F32)
        nc.vector.tensor_tensor(out=csq[:], in0=c_sb[:], in1=c_sb[:], op=ALU.mult)
        cvs = keep.tile([P, NCODE], F32)
        nc.vector.tensor_reduce(
            out=cvs[:], in_=csq[:].rearrange("p t c -> p c t"), axis=AX.X, op=ALU.add
        )
        w2g = keep.tile([P, CF, 4], BF16, align_bytes=64)
        regroup(nc.scalar.copy, w2g[:], w2_raw[:])
        hpT_sb = keep.tile([P, 4, TOK], F32)
        for t in range(4):
            nc.vector.tensor_copy(out=hpT_sb[:, t, :], in_=hpT_ps[t][:])
        v_ps = pso.tile([P, NCODE], F32, tag="o")
        nc.tensor.matmul(v_ps[:], lhsT=ones[:], rhs=cvs[:], start=True, stop=False)
        for t in range(4):
            nc.tensor.matmul(v_ps[:], lhsT=hpT_sb[:, t, :], rhs=c2[:, t, :], start=False, stop=(t == 3))

        st = keep.tile([P, 6], F32)
        nc.vector.bn_stats(out=st[:], in_=hp_ps[:])
        mv = keep.tile([P, 2], F32)
        nc.vector.bn_aggr(out=mv[:], in_=st[:])
        vhe = keep.tile([P, 1], F32)
        nc.vector.tensor_scalar_add(out=vhe[:], in0=mv[:, 1:2], scalar1=LN_EPS)
        mh_ps = pso.tile([P, TOK], F32, tag="o")
        nc.tensor.transpose(mh_ps[:], mv[:, 0:1].to_broadcast([P, P]), ident[:])
        std = keep.tile([P, NCODE], F32)
        nc.scalar.activation(out=std[:], in_=v_ps[:], func=ACT.Sqrt, bias=vhe[:, 0:1])
        nc.scalar.activation(out=warm[:], in_=eps[:], func=ACT.Tanh)
        w2_codes = keep.tile([P, CF], U32, align_bytes=64)
        w2_scales = keep.tile([P, CF], U8, align_bytes=64)
        nc.vector.quantize_mx(
            out=w2_codes[:].bitcast(FP8X4),
            scales=w2_scales[:],
            in_=w2g[:].rearrange("p c t -> p (c t)"),
        )
        r_sb = keep.tile([P, NCODE], F32)
        nc.vector.reciprocal(out=r_sb[:], in_=std[:])
        a_sb = keep.tile([P, 4, TOK], F32)
        nc.vector.tensor_tensor(
            out=a_sb[:],
            in0=hpT_sb[:],
            in1=mh_ps[:].unsqueeze(1).to_broadcast([P, 4, TOK]),
            op=ALU.subtract,
        )

        tiles = {}

        def bcast_r(rd):
            for cl in range(CG):
                code = CG * rd + cl
                if rd == 0:
                    r_one = pso.tile([P, TOK], F32, tag="o", name="r_one")
                    tiles[("r", rd, cl)] = r_one[:]
                else:
                    if cl == 0:
                        r_ps = psr.tile([P, CG, TOK], F32, tag="r", name="r_ps")
                        tiles[("rt", rd)] = r_ps
                    tiles[("r", rd, cl)] = tiles[("rt", rd)][:, cl, :]
                nc.tensor.transpose(
                    tiles[("r", rd, cl)], r_sb[:, code : code + 1].to_broadcast([P, P]), ident[:]
                )

        def normalise(rd, cls):
            if cls[0] == 0:
                z_new = work.tile([P, 4, CG, TOK], F32, name="z")
                tiles[("z", rd)] = z_new
            z = tiles[("z", rd)]
            for cl in cls:
                code = CG * rd + cl
                for t in range(4):
                    nc.vector.scalar_tensor_tensor(
                        out=z[:, t, cl, :],
                        in0=a_sb[:, t, :],
                        scalar=c_sb[:, t, code : code + 1],
                        in1=tiles[("r", rd, cl)],
                        op0=ALU.add,
                        op1=ALU.mult,
                    )

        def gain_bias(rd, chunks, eng):
            z = tiles[("z", rd)]
            if ("m", rd) not in tiles:
                m_new = work.tile([P, 4, W], BF16, name="m")
                tiles[("m", rd)] = m_new
            m = tiles[("m", rd)]
            for t in chunks:
                if eng == "s":
                    nc.scalar.activation(
                        out=m[:, t, :],
                        in_=z[:, t].rearrange("p c r -> p (c r)"),
                        func=ACT.Identity,
                        scale=smT[:, t, ROW_G : ROW_G + 1],
                        bias=smT[:, t, ROW_B : ROW_B + 1],
                    )
                else:
                    engine = nc.gpsimd if eng == "g" else nc.vector
                    engine.tensor_scalar(
                        out=m[:, t, :],
                        in0=z[:, t].rearrange("p c r -> p (c r)"),
                        scalar1=smT[:, t, ROW_G : ROW_G + 1],
                        scalar2=smT[:, t, ROW_B : ROW_B + 1],
                        op0=ALU.mult,
                        op1=ALU.add,
                    )

        def regroup_mu(rd, vector_rows):
            m = tiles[("m", rd)]
            mg = work.tile([P, W, 4], BF16, align_bytes=64, name="mg")
            tiles[("mg", rd)] = mg
            if vector_rows > 0:
                regroup(nc.vector.tensor_copy, mg[:, 0:vector_rows], m[:, :, 0:vector_rows])
            regroup(nc.scalar.copy, mg[:, vector_rows:W], m[:, :, vector_rows:W])

        def quantise_mu(rd):
            mg = tiles[("mg", rd)]
            mu_codes = work.tile([P, W], U32, align_bytes=64, name="mu_codes")
            mu_scales = work.tile([P, W], U8, align_bytes=64, name="mu_scales")
            tiles[("q", rd)] = (mu_codes, mu_scales)
            nc.vector.quantize_mx(
                out=mu_codes[:].bitcast(FP8X4),
                scales=mu_scales[:],
                in_=mg[:].rearrange("p w t -> p (w t)"),
            )

        def second_mm(rd):
            mu_codes, mu_scales = tiles[("q", rd)]
            for cl in range(CG):
                o_ps = pso.tile([P, CF], F32, tag="o", name="o_ps")
                tiles[("o", rd, cl)] = o_ps
                nc.tensor.matmul_mx(
                    out=o_ps[:],
                    lhsT=mu_codes[:, TOK * cl : TOK * (cl + 1)].bitcast(FP8X4),
                    lhsT_scale=mu_scales[:, TOK * cl : TOK * (cl + 1)],
                    rhs=w2_codes[:].bitcast(FP8X4),
                    rhs_scale=w2_scales[:],
                    start=True,
                    stop=True,
                )

        def finish(rd, cls, lo=0, hi=CF):
            if ("res", rd) not in tiles:
                res_new = work.tile([P, CG, CF], F32, name="res")
                tiles[("res", rd)] = res_new
            res = tiles[("res", rd)]
            for cl in cls:
                nc.vector.tensor_tensor(
                    out=res[:, cl, lo:hi],
                    in0=tiles[("o", rd, cl)][:, lo:hi],
                    in1=b2_bc[:, lo:hi],
                    op=ALU.add,
                )
            for cl in cls:
                nc.scalar.activation(out=res[:, cl, lo:hi], in_=res[:, cl, lo:hi], func=ACT.Tanh)
            c0 = CG * rd + cls[0]
            c1 = CG * rd + cls[-1] + 1
            nc.sync.dma_start(
                out=out3[:, c0:c1, lo:hi], in_=res[:, cls[0] : cls[-1] + 1, lo:hi]
            )

        for rd in range(LEAD + 1):
            bcast_r(rd)
        normalise(0, [0, 1, 2, 3])
        gain_bias(0, [0, 1], "s")
        gain_bias(0, [2, 3], "g")
        normalise(1, [0, 1, 2, 3])
        gain_bias(1, [2, 3], "g")
        for rd in range(ROUNDS):
            nxt = rd + LEAD
            more = nxt < ROUNDS
            if nxt + 1 < ROUNDS:
                bcast_r(nxt + 1)
            regroup_mu(rd, W // 2 if rd == ROUNDS - 1 else 0)
            if rd == 0:
                gain_bias(1, [0, 1], "s")
            if more:
                normalise(nxt, [0])
            if rd > 0:
                finish(rd - 1, [0, 1, 2, 3])
            if more:
                normalise(nxt, [1, 2])
            quantise_mu(rd)
            second_mm(rd)
            if more:
                normalise(nxt, [3])
                if nxt == ROUNDS - 1:
                    gain_bias(nxt, [0, 1], "v")
                    gain_bias(nxt, [2, 3], "g")
                else:
                    gain_bias(nxt, [0, 1, 2, 3], "g")
        last = ROUNDS - 1
        finish(last, [0, 1])
        finish(last, [2])
        finish(last, [3], 0, CF // 2)
        finish(last, [3], CF // 2, CF)
